import numpy as np
import ml_dtypes


BF16 = ml_dtypes.bfloat16


def bf(x):
    return np.asarray(x, np.float32).astype(BF16)


def f64(x):
    return np.asarray(x).astype(np.float64)


E2M1 = np.array([0.0, 0.5, 1.0, 1.5, 2.0, 3.0, 4.0, 6.0, -0.0, -0.5, -1.0, -1.5, -2.0, -3.0, -4.0, -6.0])


def pack_weight(w, fmt):
    k, n = w.shape
    w = f64(bf(w)).reshape(k // 32, 32, n)
    amax = np.abs(w).max(1)
    if fmt == "e4m3":
        byte = np.frexp(amax)[1] - 1 + 127 - 7
    else:
        mant, ex = np.frexp(amax / 6.0)
        byte = np.where(mant > 0.5, ex, ex - 1) + 127
    byte = np.clip(np.where(amax > 0, byte, 1), 1, 254)
    scaled = (w * np.exp2(127.0 - byte)[:, None, :]).reshape(k, n).astype(np.float32)
    by_word = np.ascontiguousarray(scaled.reshape(k // 512, 128, 4, n).transpose(0, 1, 3, 2))
    if fmt == "e4m3":
        words = by_word.astype(ml_dtypes.float8_e4m3fn).view(np.uint8)
    else:
        c = by_word.astype(ml_dtypes.float4_e2m1fn).view(np.uint8) & 0xF
        words = c[..., 0::2] | (c[..., 1::2] << 4)
    return np.ascontiguousarray(words), np.ascontiguousarray(byte.astype(np.uint8).reshape(k // 512, 16, n))


def unpack_weight(words, scales, fmt):
    g, p, n, _ = words.shape
    if fmt == "e4m3":
        vals = np.ascontiguousarray(words).view(ml_dtypes.float8_e4m3fn).astype(np.float64)
    else:
        nib = np.empty((g, p, n, 4), np.uint8)
        nib[..., 0::2] = words & 0xF
        nib[..., 1::2] = words >> 4
        vals = E2M1[nib]
    vals = vals * np.repeat(np.exp2(scales.astype(np.float64) - 127.0), 8, axis=1)[..., None]
    return vals.transpose(0, 1, 3, 2).reshape(g * 512, n)

def pack4(w):
    words, scales = pack_weight(w, "e2m1")
    return words.reshape(words.shape[0], 128, -1), scales


def unpack4(words, scales):
    return unpack_weight(words.reshape(words.shape[0], 128, -1, 2), scales, "e2m1")


def kspread(k):
    return np.exp2(np.repeat(np.random.randint(-6, 7, k // 32), 32).astype(np.float64))


B, S, D, NH, NKV, HD, QB = 1, 128, 8192, 16, 4, 128, 512
Q_DIM = NH * HD
KV_DIM = NKV * HD


def rot(t, f0, f1):
    tp = t.reshape(t.shape[:-1] + (HD // 2, 2))
    t0, t1 = tp[..., 0], tp[..., 1]
    row1 = t0 * f0 + t1 * f1
    row0 = t0 * f1 - t1 * f0
    return np.stack([row0, row1], axis=-1).reshape(t.shape)


def setup_inputs():
    s = kspread(D)
    x = np.random.standard_normal((B, S, D)) * s
    x_words, x_scales = pack4(np.ascontiguousarray(x.reshape(B * S, D).T))
    freqs_cis = bf(np.random.standard_normal((S, HD)))
    w = np.random.standard_normal((Q_DIM + 2 * KV_DIM, D)) / np.sqrt(D) / s
    words, scales = pack4(np.ascontiguousarray(w.T))
    return {"x_words": x_words,
            "x_scales": x_scales,
            "freqs_cis": freqs_cis,
            "Wqkv_words": words,
            "Wqkv_scales": scales}


def reference(x_words, x_scales, freqs_cis, Wqkv_words, Wqkv_scales):
    xqkv = unpack4(x_words, x_scales).T.reshape(B, S, D) @ unpack4(Wqkv_words, Wqkv_scales)
    xq = xqkv[..., :Q_DIM].reshape(B, S, NH, HD)
    xk = xqkv[..., Q_DIM:Q_DIM + KV_DIM].reshape(B, S, NKV, HD)
    xv = xqkv[..., Q_DIM + KV_DIM:].reshape(B, S, NKV, HD)
    f = f64(freqs_cis).reshape(S, 1, HD // 2, 2)
    f0, f1 = f[..., 0], f[..., 1]
    q_rot = rot(xq, f0, f1).transpose(0, 2, 1, 3)
    k_rot = rot(xk, f0, f1).transpose(0, 2, 1, 3)
    v = xv.transpose(0, 2, 1, 3)
    return q_rot, k_rot, v

@@ -1,0 +1,166 @@
+from contextlib import ExitStack
+
+import concourse.mybir as mybir
+
+F32 = mybir.dt.float32
+BF16 = mybir.dt.bfloat16
+U8 = mybir.dt.uint8
+I32 = mybir.dt.int32
+FP4X4 = mybir.dt.float4_e2m1fn_x4
+MULT = mybir.AluOpType.mult
+ADD = mybir.AluOpType.add
+
+P = 128
+PASSES = 16
+N_ALL = 3072
+BLOCK = 512
+Q_COLS = 2048
+KV_COLS = 1024
+
+FLOPS = 2 * 128 * 8192 * 3072
+
+SCALE_GROUPS = (2, 2, 2, 2, 2, 2, 2, 1, 1)
+Q_LOAD_PASSES = 2
+KV_LOADS = (4, 4, 4, 2, 1, 1)
+
+
+def tile_rlaattention_pa_kernel(
+    tc, x_words, x_scales, freqs_cis, Wqkv_words, Wqkv_scales, out_0, out_1, out_2
+):
+    nc = tc.nc
+    with ExitStack() as ctx:
+        keep = ctx.enter_context(tc.tile_pool(name="keep", bufs=1))
+        work = ctx.enter_context(tc.tile_pool(name="work", bufs=3))
+        psum = ctx.enter_context(tc.psum_pool(name="psum", bufs=1))
+        ctx.enter_context(tc.manual_schedule())
+
+        fr = keep.tile([P, 128], BF16, name="fr")
+        nc.scalar.dma_start(out=fr[:], in_=freqs_cis)
+
+        xc = keep.tile([P, PASSES, 256], U8, name="xc", align_bytes=64)
+        nc.sync.dma_start(
+            out=xc[:].bitcast(I32), in_=x_words.rearrange("g p n -> p g n").bitcast(I32)
+        )
+
+        def load_scale_rows(plane, rows):
+            nc.vector.memset(plane[:].bitcast(I32), 0)
+            for r in range(4):
+                nc.sync.dma_start(
+                    out=plane[r:P:32, :, :].bitcast(I32),
+                    in_=rows[:, r:16:4, :].rearrange("g q n -> q g n").bitcast(I32),
+                )
+
+        xs = keep.tile([P, PASSES, 128], U8, name="xs", align_bytes=64)
+        load_scale_rows(xs, x_scales)
+
+        ws = {}
+        g0 = 0
+        for t, n in enumerate(SCALE_GROUPS):
+            plane = keep.tile([P, n, N_ALL], U8, name="ws%d" % t, align_bytes=64)
+            load_scale_rows(plane, Wqkv_scales[g0 : g0 + n])
+            for s in range(n):
+                ws[g0 + s] = plane[:, s, :]
+            g0 += n
+
+        wq = []
+        for i in range(PASSES // Q_LOAD_PASSES):
+            codes = keep.tile([P, Q_LOAD_PASSES, 2 * Q_COLS], U8, name="wq%d" % i, align_bytes=64)
+            nc.sync.dma_start(
+                out=codes[:].bitcast(I32),
+                in_=Wqkv_words[i * Q_LOAD_PASSES : (i + 1) * Q_LOAD_PASSES, :, 0 : 2 * Q_COLS]
+                .rearrange("g p n -> p g n")
+                .bitcast(I32),
+            )
+            wq.append(codes)
+
+        wkv = {}
+        g0 = 0
+        for i, n in enumerate(KV_LOADS):
+            codes = keep.tile([P, n, 2 * KV_COLS], U8, name="wkv%d" % i, align_bytes=64)
+            nc.sync.dma_start(
+                out=codes[:].bitcast(I32),
+                in_=Wqkv_words[g0 : g0 + n, :, 2 * Q_COLS : 2 * N_ALL]
+                .rearrange("g p n -> p g n")
+                .bitcast(I32),
+            )
+            for s in range(n):
+                wkv[g0 + s] = codes[:, s, :]
+            g0 += n
+
+        fa = keep.tile([P, BLOCK], F32, name="fa")
+        fb = keep.tile([P, BLOCK], F32, name="fb")
+        fr3 = fr[:].rearrange("p (j t) -> p j t", t=2)
+        fa3 = fa[:, 0:128].rearrange("p (j t) -> p j t", t=2)
+        fb3 = fb[:, 0:128].rearrange("p (j t) -> p j t", t=2)
+        nc.scalar.copy(out=fa3[:, :, 0], in_=fr3[:, :, 1])
+        nc.scalar.copy(out=fa3[:, :, 1], in_=fr3[:, :, 1])
+        nc.scalar.copy(out=fb3[:, :, 0], in_=fr3[:, :, 0])
+        nc.scalar.mul(out=fb3[:, :, 1], in_=fr3[:, :, 0], mul=-1.0)
+        for tab in (fa, fb):
+            nc.scalar.copy(out=tab[:, 128:256], in_=tab[:, 0:128])
+            nc.scalar.copy(out=tab[:, 256:512], in_=tab[:, 0:256])
+
+        def multiply(acc, g, codes, col0):
+            nc.tensor.matmul_mx(
+                out=acc[:],
+                lhsT=xc[:, g, :].bitcast(FP4X4),
+                lhsT_scale=xs[:, g, :],
+                rhs=codes.bitcast(FP4X4),
+                rhs_scale=ws[g][:, col0 : col0 + BLOCK],
+                start=(g == 0),
+                stop=(g == PASSES - 1),
+            )
+
+        acc = [psum.tile([P, BLOCK], F32, name="acc%d" % j) for j in range(6)]
+        for g in range(PASSES):
+            for j in range(4):
+                multiply(
+                    acc[j],
+                    g,
+                    wq[g // Q_LOAD_PASSES][:, g % Q_LOAD_PASSES, 2 * BLOCK * j : 2 * BLOCK * (j + 1)],
+                    BLOCK * j,
+                )
+        for g in range(PASSES):
+            for j in (4, 5):
+                multiply(
+                    acc[j], g, wkv[g][:, 2 * BLOCK * (j - 4) : 2 * BLOCK * (j - 3)], BLOCK * j
+                )
+
+        res = [keep.tile([P, BLOCK], F32, name="res%d" % j) for j in range(6)]
+        prods = {}
+
+        def products(j):
+            m1 = work.tile([P, BLOCK], F32, name="m1")
+            m2 = work.tile([P, BLOCK], F32, name="m2")
+            nc.vector.tensor_tensor(out=m1[:], in0=acc[j][:], in1=fa[:], op=MULT)
+            nc.vector.tensor_tensor(out=m2[:], in0=acc[j][:], in1=fb[:], op=MULT)
+            prods[j] = (m1, m2)
+
+        def combine(j):
+            m1, m2 = prods[j]
+            nc.vector.tensor_tensor(
+                out=res[j][:].rearrange("p (j t) -> p j t", t=2),
+                in0=m1[:].rearrange("p (j t) -> p j t", t=2),
+                in1=m2[:].rearrange("p (j t) -> p j t", t=2)[:, :, ::-1],
+                op=ADD,
+            )
+
+        products(0)
+        for j in range(1, 4):
+            products(j)
+            combine(j - 1)
+        combine(3)
+        products(4)
+        combine(4)
+        nc.scalar.copy(out=res[5][:], in_=acc[5][:])
+
+        def store(dst, j):
+            nc.sync.dma_start(
+                out=dst.rearrange("h p f -> p h f"),
+                in_=res[j][:].rearrange("p (h f) -> p h f", h=4),
+            )
+
+        for j in range(4):
+            store(out_0[0, 4 * j : 4 * j + 4], j)
+        store(out_2[0], 5)
+        store(out_1[0], 4)

@@ -20,8 +20,12 @@ KV_COLS = 1024
 FLOPS = 2 * 128 * 8192 * 3072
 
 SCALE_GROUPS = (2, 2, 2, 2, 2, 2, 2, 1, 1)
-Q_LOAD_PASSES = 2
-KV_LOADS = (4, 4, 4, 2, 1, 1)
+Q_LOAD_PASSES = 1
+KV_LOADS = (1,) * 16
+WARM_GROUP = 5
+WARM_MATMULS = 8
+V_LAG = 2
+HALF = 256
 
 
 def tile_rlaattention_pa_kernel(
@@ -61,6 +65,8 @@ def tile_rlaattention_pa_kernel(
             for s in range(n):
                 ws[g0 + s] = plane[:, s, :]
             g0 += n
+            if t == WARM_GROUP:
+                warm_plane = plane
 
         wq = []
         for i in range(PASSES // Q_LOAD_PASSES):
@@ -87,6 +93,10 @@ def tile_rlaattention_pa_kernel(
                 wkv[g0 + s] = codes[:, s, :]
             g0 += n
 
+        zeros = keep.tile([P, 128 + BLOCK], BF16, name="zeros")
+        nc.vector.tensor_copy(out=zeros[:, 0:32].bitcast(U8), in_=warm_plane[:, 0, 0:64])
+        nc.vector.memset(zeros[:], 0.0)
+
         fa = keep.tile([P, BLOCK], F32, name="fa")
         fb = keep.tile([P, BLOCK], F32, name="fb")
         fr3 = fr[:].rearrange("p (j t) -> p j t", t=2)
@@ -112,6 +122,11 @@ def tile_rlaattention_pa_kernel(
             )
 
         acc = [psum.tile([P, BLOCK], F32, name="acc%d" % j) for j in range(6)]
+        junk = psum.tile([P, BLOCK], F32, name="junk")
+        for i in range(WARM_MATMULS):
+            nc.tensor.matmul(
+                out=junk[:], lhsT=zeros[:, 0:128], rhs=zeros[:, 128 : 128 + BLOCK], start=True, stop=True
+            )
         for g in range(PASSES):
             for j in range(4):
                 multiply(
@@ -120,47 +135,50 @@ def tile_rlaattention_pa_kernel(
                     wq[g // Q_LOAD_PASSES][:, g % Q_LOAD_PASSES, 2 * BLOCK * j : 2 * BLOCK * (j + 1)],
                     BLOCK * j,
                 )
-        for g in range(PASSES):
-            for j in (4, 5):
-                multiply(
-                    acc[j], g, wkv[g][:, 2 * BLOCK * (j - 4) : 2 * BLOCK * (j - 3)], BLOCK * j
-                )
+        for g in range(PASSES + V_LAG):
+            if g < PASSES:
+                multiply(acc[4], g, wkv[g][:, 0 : 2 * BLOCK], BLOCK * 4)
+            if g >= V_LAG:
+                multiply(acc[5], g - V_LAG, wkv[g - V_LAG][:, 2 * BLOCK : 4 * BLOCK], BLOCK * 5)
 
         res = [keep.tile([P, BLOCK], F32, name="res%d" % j) for j in range(6)]
         prods = {}
 
-        def products(j):
+        def products(j, c0, c1):
             m1 = work.tile([P, BLOCK], F32, name="m1")
             m2 = work.tile([P, BLOCK], F32, name="m2")
-            nc.vector.tensor_tensor(out=m1[:], in0=acc[j][:], in1=fa[:], op=MULT)
-            nc.vector.tensor_tensor(out=m2[:], in0=acc[j][:], in1=fb[:], op=MULT)
-            prods[j] = (m1, m2)
+            nc.vector.tensor_tensor(out=m1[:, c0:c1], in0=acc[j][:, c0:c1], in1=fa[:, c0:c1], op=MULT)
+            nc.vector.tensor_tensor(out=m2[:, c0:c1], in0=acc[j][:, c0:c1], in1=fb[:, c0:c1], op=MULT)
+            prods[(j, c0)] = (m1, m2)
 
-        def combine(j):
-            m1, m2 = prods[j]
+        def combine(j, c0, c1):
+            m1, m2 = prods[(j, c0)]
             nc.vector.tensor_tensor(
-                out=res[j][:].rearrange("p (j t) -> p j t", t=2),
-                in0=m1[:].rearrange("p (j t) -> p j t", t=2),
-                in1=m2[:].rearrange("p (j t) -> p j t", t=2)[:, :, ::-1],
+                out=res[j][:, c0:c1].rearrange("p (j t) -> p j t", t=2),
+                in0=m1[:, c0:c1].rearrange("p (j t) -> p j t", t=2),
+                in1=m2[:, c0:c1].rearrange("p (j t) -> p j t", t=2)[:, :, ::-1],
                 op=ADD,
             )
 
-        products(0)
-        for j in range(1, 4):
-            products(j)
-            combine(j - 1)
-        combine(3)
-        products(4)
-        combine(4)
-        nc.scalar.copy(out=res[5][:], in_=acc[5][:])
-
-        def store(dst, j):
-            nc.sync.dma_start(
+        def store(queue, dst, j, c0, c1):
+            queue.dma_start(
                 out=dst.rearrange("h p f -> p h f"),
-                in_=res[j][:].rearrange("p (h f) -> p h f", h=4),
+                in_=res[j][:, c0:c1].rearrange("p (h f) -> p h f", f=128),
             )
 
+        products(0, 0, BLOCK)
+        for j in range(1, 4):
+            products(j, 0, BLOCK)
+            combine(j - 1, 0, BLOCK)
+        combine(3, 0, BLOCK)
         for j in range(4):
-            store(out_0[0, 4 * j : 4 * j + 4], j)
-        store(out_2[0], 5)
-        store(out_1[0], 4)
+            store(nc.sync, out_0[0, 4 * j : 4 * j + 4], j, 0, BLOCK)
+
+        products(4, 0, HALF)
+        products(4, HALF, BLOCK)
+        for h in range(2):
+            combine(4, h * HALF, (h + 1) * HALF)
+            store(nc.sync, out_1[0, 2 * h : 2 * h + 2], 4, h * HALF, (h + 1) * HALF)
+        for h in range(2):
+            nc.scalar.copy(out=res[5][:, h * HALF : (h + 1) * HALF], in_=acc[5][:, h * HALF : (h + 1) * HALF])
+            store(nc.scalar, out_2[0, 2 * h : 2 * h + 2], 5, h * HALF, (h + 1) * HALF)

@@ -19,11 +19,9 @@ KV_COLS = 1024
 
 FLOPS = 2 * 128 * 8192 * 3072
 
-SCALE_GROUPS = (2, 2, 2, 2, 2, 2, 2, 1, 1)
+SCALE_GROUPS = (4, 4, 4, 2, 2)
 Q_LOAD_PASSES = 1
 KV_LOADS = (1,) * 16
-WARM_GROUP = 5
-WARM_MATMULS = 8
 V_LAG = 2
 HALF = 256
 
@@ -46,27 +44,28 @@ def tile_rlaattention_pa_kernel(
             out=xc[:].bitcast(I32), in_=x_words.rearrange("g p n -> p g n").bitcast(I32)
         )
 
-        def load_scale_rows(plane, rows):
+        def load_scale_rows(plane, rows, apart):
             nc.vector.memset(plane[:].bitcast(I32), 0)
-            for r in range(4):
-                nc.sync.dma_start(
-                    out=plane[r:P:32, :, :].bitcast(I32),
-                    in_=rows[:, r:16:4, :].rearrange("g q n -> q g n").bitcast(I32),
-                )
+            for quad in range(apart // 32):
+                for r in range(4):
+                    nc.sync.dma_start(
+                        out=plane[32 * quad + r : P : apart, :, :].bitcast(I32),
+                        in_=rows[:, 4 * quad + r : 16 : apart // 8, :]
+                        .rearrange("g q n -> q g n")
+                        .bitcast(I32),
+                    )
 
         xs = keep.tile([P, PASSES, 128], U8, name="xs", align_bytes=64)
-        load_scale_rows(xs, x_scales)
+        load_scale_rows(xs, x_scales, 32)
 
         ws = {}
         g0 = 0
         for t, n in enumerate(SCALE_GROUPS):
             plane = keep.tile([P, n, N_ALL], U8, name="ws%d" % t, align_bytes=64)
-            load_scale_rows(plane, Wqkv_scales[g0 : g0 + n])
+            load_scale_rows(plane, Wqkv_scales[g0 : g0 + n], 64)
             for s in range(n):
                 ws[g0 + s] = plane[:, s, :]
             g0 += n
-            if t == WARM_GROUP:
-                warm_plane = plane
 
         wq = []
         for i in range(PASSES // Q_LOAD_PASSES):
@@ -93,10 +92,6 @@ def tile_rlaattention_pa_kernel(
                 wkv[g0 + s] = codes[:, s, :]
             g0 += n
 
-        zeros = keep.tile([P, 128 + BLOCK], BF16, name="zeros")
-        nc.vector.tensor_copy(out=zeros[:, 0:32].bitcast(U8), in_=warm_plane[:, 0, 0:64])
-        nc.vector.memset(zeros[:], 0.0)
-
         fa = keep.tile([P, BLOCK], F32, name="fa")
         fb = keep.tile([P, BLOCK], F32, name="fb")
         fr3 = fr[:].rearrange("p (j t) -> p j t", t=2)
@@ -122,11 +117,6 @@ def tile_rlaattention_pa_kernel(
             )
 
         acc = [psum.tile([P, BLOCK], F32, name="acc%d" % j) for j in range(6)]
-        junk = psum.tile([P, BLOCK], F32, name="junk")
-        for i in range(WARM_MATMULS):
-            nc.tensor.matmul(
-                out=junk[:], lhsT=zeros[:, 0:128], rhs=zeros[:, 128 : 128 + BLOCK], start=True, stop=True
-            )
         for g in range(PASSES):
             for j in range(4):
                 multiply(

@@ -162,7 +162,7 @@ def tile_rlaattention_pa_kernel(
             combine(j - 1, 0, BLOCK)
         combine(3, 0, BLOCK)
         for j in range(4):
-            store(nc.sync, out_0[0, 4 * j : 4 * j + 4], j, 0, BLOCK)
+            store((nc.sync, nc.scalar)[j % 2], out_0[0, 4 * j : 4 * j + 4], j, 0, BLOCK)
 
         products(4, 0, HALF)
         products(4, HALF, BLOCK)

@@ -22,8 +22,6 @@ FLOPS = 2 * 128 * 8192 * 3072
 SCALE_GROUPS = (4, 4, 4, 2, 2)
 Q_LOAD_PASSES = 1
 KV_LOADS = (1,) * 16
-V_LAG = 2
-HALF = 256
 
 
 def tile_rlaattention_pa_kernel(
@@ -125,50 +123,47 @@ def tile_rlaattention_pa_kernel(
                     wq[g // Q_LOAD_PASSES][:, g % Q_LOAD_PASSES, 2 * BLOCK * j : 2 * BLOCK * (j + 1)],
                     BLOCK * j,
                 )
-        for g in range(PASSES + V_LAG):
-            if g < PASSES:
-                multiply(acc[4], g, wkv[g][:, 0 : 2 * BLOCK], BLOCK * 4)
-            if g >= V_LAG:
-                multiply(acc[5], g - V_LAG, wkv[g - V_LAG][:, 2 * BLOCK : 4 * BLOCK], BLOCK * 5)
+        for g in range(PASSES):
+            for j in (4, 5):
+                multiply(
+                    acc[j], g, wkv[g][:, 2 * BLOCK * (j - 4) : 2 * BLOCK * (j - 3)], BLOCK * j
+                )
 
         res = [keep.tile([P, BLOCK], F32, name="res%d" % j) for j in range(6)]
         prods = {}
 
-        def products(j, c0, c1):
+        def products(j):
             m1 = work.tile([P, BLOCK], F32, name="m1")
             m2 = work.tile([P, BLOCK], F32, name="m2")
-            nc.vector.tensor_tensor(out=m1[:, c0:c1], in0=acc[j][:, c0:c1], in1=fa[:, c0:c1], op=MULT)
-            nc.vector.tensor_tensor(out=m2[:, c0:c1], in0=acc[j][:, c0:c1], in1=fb[:, c0:c1], op=MULT)
-            prods[(j, c0)] = (m1, m2)
+            nc.vector.tensor_tensor(out=m1[:], in0=acc[j][:], in1=fa[:], op=MULT)
+            nc.vector.tensor_tensor(out=m2[:], in0=acc[j][:], in1=fb[:], op=MULT)
+            prods[j] = (m1, m2)
 
-        def combine(j, c0, c1):
-            m1, m2 = prods[(j, c0)]
+        def combine(j):
+            m1, m2 = prods[j]
             nc.vector.tensor_tensor(
-                out=res[j][:, c0:c1].rearrange("p (j t) -> p j t", t=2),
-                in0=m1[:, c0:c1].rearrange("p (j t) -> p j t", t=2),
-                in1=m2[:, c0:c1].rearrange("p (j t) -> p j t", t=2)[:, :, ::-1],
+                out=res[j][:].rearrange("p (j t) -> p j t", t=2),
+                in0=m1[:].rearrange("p (j t) -> p j t", t=2),
+                in1=m2[:].rearrange("p (j t) -> p j t", t=2)[:, :, ::-1],
                 op=ADD,
             )
 
-        def store(queue, dst, j, c0, c1):
-            queue.dma_start(
+        products(0)
+        for j in range(1, 4):
+            products(j)
+            combine(j - 1)
+        combine(3)
+        products(4)
+        combine(4)
+        nc.scalar.copy(out=res[5][:], in_=acc[5][:])
+
+        def store(dst, j):
+            nc.sync.dma_start(
                 out=dst.rearrange("h p f -> p h f"),
-                in_=res[j][:, c0:c1].rearrange("p (h f) -> p h f", f=128),
+                in_=res[j][:].rearrange("p (h f) -> p h f", h=4),
             )
 
-        products(0, 0, BLOCK)
-        for j in range(1, 4):
-            products(j, 0, BLOCK)
-            combine(j - 1, 0, BLOCK)
-        combine(3, 0, BLOCK)
         for j in range(4):
-            store((nc.sync, nc.scalar)[j % 2], out_0[0, 4 * j : 4 * j + 4], j, 0, BLOCK)
-
-        products(4, 0, HALF)
-        products(4, HALF, BLOCK)
-        for h in range(2):
-            combine(4, h * HALF, (h + 1) * HALF)
-            store(nc.sync, out_1[0, 2 * h : 2 * h + 2], 4, h * HALF, (h + 1) * HALF)
-        for h in range(2):
-            nc.scalar.copy(out=res[5][:, h * HALF : (h + 1) * HALF], in_=acc[5][:, h * HALF : (h + 1) * HALF])
-            store(nc.scalar, out_2[0, 2 * h : 2 * h + 2], 5, h * HALF, (h + 1) * HALF)
+            store(out_0[0, 4 * j : 4 * j + 4], j)
+        store(out_2[0], 5)
+        store(out_1[0], 4)

@@ -19,7 +19,7 @@ KV_COLS = 1024
 
 FLOPS = 2 * 128 * 8192 * 3072
 
-SCALE_GROUPS = (4, 4, 4, 2, 2)
+SCALE_GROUPS = (8, 8)
 Q_LOAD_PASSES = 1
 KV_LOADS = (1,) * 16
 
@@ -60,7 +60,14 @@ def tile_rlaattention_pa_kernel(
         g0 = 0
         for t, n in enumerate(SCALE_GROUPS):
             plane = keep.tile([P, n, N_ALL], U8, name="ws%d" % t, align_bytes=64)
-            load_scale_rows(plane, Wqkv_scales[g0 : g0 + n], 64)
+            nc.vector.memset(plane[:].bitcast(I32), 0)
+            for low in (0, 1, 2, 3, 32, 33, 34, 35):
+                for p in (low, low + 64):
+                    q = 4 * (p // 32) + p % 32
+                    nc.sync.dma_start(
+                        out=plane[p : p + 1, :, :].bitcast(I32),
+                        in_=Wqkv_scales[g0 : g0 + n, q : q + 1, :].rearrange("g q n -> q g n").bitcast(I32),
+                    )
             for s in range(n):
                 ws[g0 + s] = plane[:, s, :]
             g0 += n

@@ -57,17 +57,25 @@ def tile_rlaattention_pa_kernel(
         load_scale_rows(xs, x_scales, 32)
 
         ws = {}
+        woven = []
+
+        def load_scale_row(plane, g0, n, p):
+            q = 4 * (p // 32) + p % 32
+            nc.sync.dma_start(
+                out=plane[p : p + 1, :, :].bitcast(I32),
+                in_=Wqkv_scales[g0 : g0 + n, q : q + 1, :].rearrange("g q n -> q g n").bitcast(I32),
+            )
+
         g0 = 0
         for t, n in enumerate(SCALE_GROUPS):
             plane = keep.tile([P, n, N_ALL], U8, name="ws%d" % t, align_bytes=64)
             nc.vector.memset(plane[:].bitcast(I32), 0)
             for low in (0, 1, 2, 3, 32, 33, 34, 35):
                 for p in (low, low + 64):
-                    q = 4 * (p // 32) + p % 32
-                    nc.sync.dma_start(
-                        out=plane[p : p + 1, :, :].bitcast(I32),
-                        in_=Wqkv_scales[g0 : g0 + n, q : q + 1, :].rearrange("g q n -> q g n").bitcast(I32),
-                    )
+                    if t == 0:
+                        load_scale_row(plane, g0, n, p)
+                    else:
+                        woven.append((plane, g0, n, p))
             for s in range(n):
                 ws[g0 + s] = plane[:, s, :]
             g0 += n
@@ -82,6 +90,8 @@ def tile_rlaattention_pa_kernel(
                 .bitcast(I32),
             )
             wq.append(codes)
+            for item in woven[2 * i : 2 * i + 2]:
+                load_scale_row(*item)
 
         wkv = {}
         g0 = 0

@@ -32,7 +32,6 @@ def tile_rlaattention_pa_kernel(
         keep = ctx.enter_context(tc.tile_pool(name="keep", bufs=1))
         work = ctx.enter_context(tc.tile_pool(name="work", bufs=3))
         psum = ctx.enter_context(tc.psum_pool(name="psum", bufs=1))
-        ctx.enter_context(tc.manual_schedule())
 
         fr = keep.tile([P, 128], BF16, name="fr")
         nc.scalar.dma_start(out=fr[:], in_=freqs_cis)

@@ -33,10 +33,10 @@ def tile_rlaattention_pa_kernel(
         work = ctx.enter_context(tc.tile_pool(name="work", bufs=3))
         psum = ctx.enter_context(tc.psum_pool(name="psum", bufs=1))
 
-        fr = keep.tile([P, 128], BF16, name="fr")
+        fr = keep.tile([P, 128], BF16, name="fr", align_bytes=256)
         nc.scalar.dma_start(out=fr[:], in_=freqs_cis)
 
-        xc = keep.tile([P, PASSES, 256], U8, name="xc", align_bytes=64)
+        xc = keep.tile([P, PASSES, 256], U8, name="xc", align_bytes=256)
         nc.sync.dma_start(
             out=xc[:].bitcast(I32), in_=x_words.rearrange("g p n -> p g n").bitcast(I32)
         )
@@ -52,7 +52,7 @@ def tile_rlaattention_pa_kernel(
                         .bitcast(I32),
                     )
 
-        xs = keep.tile([P, PASSES, 128], U8, name="xs", align_bytes=64)
+        xs = keep.tile([P, PASSES, 128], U8, name="xs", align_bytes=256)
         load_scale_rows(xs, x_scales, 32)
 
         ws = {}
@@ -67,7 +67,7 @@ def tile_rlaattention_pa_kernel(
 
         g0 = 0
         for t, n in enumerate(SCALE_GROUPS):
-            plane = keep.tile([P, n, N_ALL], U8, name="ws%d" % t, align_bytes=64)
+            plane = keep.tile([P, n, N_ALL], U8, name="ws%d" % t, align_bytes=256)
             nc.vector.memset(plane[:].bitcast(I32), 0)
             for low in (0, 1, 2, 3, 32, 33, 34, 35):
                 for p in (low, low + 64):
@@ -81,7 +81,7 @@ def tile_rlaattention_pa_kernel(
 
         wq = []
         for i in range(PASSES // Q_LOAD_PASSES):
-            codes = keep.tile([P, Q_LOAD_PASSES, 2 * Q_COLS], U8, name="wq%d" % i, align_bytes=64)
+            codes = keep.tile([P, Q_LOAD_PASSES, 2 * Q_COLS], U8, name="wq%d" % i, align_bytes=256)
             nc.sync.dma_start(
                 out=codes[:].bitcast(I32),
                 in_=Wqkv_words[i * Q_LOAD_PASSES : (i + 1) * Q_LOAD_PASSES, :, 0 : 2 * Q_COLS]
@@ -95,7 +95,7 @@ def tile_rlaattention_pa_kernel(
         wkv = {}
         g0 = 0
         for i, n in enumerate(KV_LOADS):
-            codes = keep.tile([P, n, 2 * KV_COLS], U8, name="wkv%d" % i, align_bytes=64)
+            codes = keep.tile([P, n, 2 * KV_COLS], U8, name="wkv%d" % i, align_bytes=256)
             nc.sync.dma_start(
                 out=codes[:].bitcast(I32),
                 in_=Wqkv_words[g0 : g0 + n, :, 2 * Q_COLS : 2 * N_ALL]
@@ -145,7 +145,7 @@ def tile_rlaattention_pa_kernel(
                     acc[j], g, wkv[g][:, 2 * BLOCK * (j - 4) : 2 * BLOCK * (j - 3)], BLOCK * j
                 )
 
-        res = [keep.tile([P, BLOCK], F32, name="res%d" % j) for j in range(6)]
+        res = [keep.tile([P, BLOCK], F32, name="res%d" % j, align_bytes=256) for j in range(6)]
         prods = {}
 
         def products(j):

@@ -21,7 +21,8 @@ FLOPS = 2 * 128 * 8192 * 3072
 
 SCALE_GROUPS = (8, 8)
 Q_LOAD_PASSES = 1
-KV_LOADS = (1,) * 16
+KV_WHOLE = 12
+LATE_LOADS = (3, 1)
 
 
 def tile_rlaattention_pa_kernel(
@@ -93,18 +94,26 @@ def tile_rlaattention_pa_kernel(
                 load_scale_row(*item)
 
         wkv = {}
-        g0 = 0
-        for i, n in enumerate(KV_LOADS):
-            codes = keep.tile([P, n, 2 * KV_COLS], U8, name="wkv%d" % i, align_bytes=256)
+        for g in range(KV_WHOLE):
+            codes = keep.tile([P, 2 * KV_COLS], U8, name="wkv%d" % g, align_bytes=256)
             nc.sync.dma_start(
-                out=codes[:].bitcast(I32),
-                in_=Wqkv_words[g0 : g0 + n, :, 2 * Q_COLS : 2 * N_ALL]
-                .rearrange("g p n -> p g n")
-                .bitcast(I32),
+                out=codes[:].bitcast(I32), in_=Wqkv_words[g, :, 2 * Q_COLS : 2 * N_ALL].bitcast(I32)
             )
-            for s in range(n):
-                wkv[g0 + s] = codes[:, s, :]
-            g0 += n
+            for j in (4, 5):
+                wkv[(g, j)] = codes[:, 2 * BLOCK * (j - 4) : 2 * BLOCK * (j - 3)]
+        for j in (4, 5):
+            g0 = KV_WHOLE
+            for n in LATE_LOADS:
+                codes = keep.tile([P, n, 2 * BLOCK], U8, name="late%d_%d" % (j, g0), align_bytes=256)
+                nc.sync.dma_start(
+                    out=codes[:].bitcast(I32),
+                    in_=Wqkv_words[g0 : g0 + n, :, 2 * BLOCK * j : 2 * BLOCK * (j + 1)]
+                    .rearrange("g p n -> p g n")
+                    .bitcast(I32),
+                )
+                for s in range(n):
+                    wkv[(g0 + s, j)] = codes[:, s, :]
+                g0 += n
 
         fa = keep.tile([P, BLOCK], F32, name="fa")
         fb = keep.tile([P, BLOCK], F32, name="fb")
@@ -139,11 +148,12 @@ def tile_rlaattention_pa_kernel(
                     wq[g // Q_LOAD_PASSES][:, g % Q_LOAD_PASSES, 2 * BLOCK * j : 2 * BLOCK * (j + 1)],
                     BLOCK * j,
                 )
-        for g in range(PASSES):
+        for g in range(KV_WHOLE):
             for j in (4, 5):
-                multiply(
-                    acc[j], g, wkv[g][:, 2 * BLOCK * (j - 4) : 2 * BLOCK * (j - 3)], BLOCK * j
-                )
+                multiply(acc[j], g, wkv[(g, j)], BLOCK * j)
+        for j in (4, 5):
+            for g in range(KV_WHOLE, PASSES):
+                multiply(acc[j], g, wkv[(g, j)], BLOCK * j)
 
         res = [keep.tile([P, BLOCK], F32, name="res%d" % j, align_bytes=256) for j in range(6)]
         prods = {}
@@ -173,13 +183,13 @@ def tile_rlaattention_pa_kernel(
         combine(4)
         nc.scalar.copy(out=res[5][:], in_=acc[5][:])
 
-        def store(dst, j):
-            nc.sync.dma_start(
+        def store(dst, j, queue):
+            queue.dma_start(
                 out=dst.rearrange("h p f -> p h f"),
                 in_=res[j][:].rearrange("p (h f) -> p h f", h=4),
             )
 
         for j in range(4):
-            store(out_0[0, 4 * j : 4 * j + 4], j)
-        store(out_2[0], 5)
-        store(out_1[0], 4)
+            store(out_0[0, 4 * j : 4 * j + 4], j, nc.sync)
+        store(out_1[0], 4, nc.sync)
+        store(out_2[0], 5, nc.scalar)

@@ -21,8 +21,8 @@ FLOPS = 2 * 128 * 8192 * 3072
 
 SCALE_GROUPS = (8, 8)
 Q_LOAD_PASSES = 1
-KV_WHOLE = 12
-LATE_LOADS = (3, 1)
+KV_WHOLE = 10
+LATE_LOADS = (3, 2, 1)
 
 
 def tile_rlaattention_pa_kernel(
@@ -128,18 +128,28 @@ def tile_rlaattention_pa_kernel(
             nc.scalar.copy(out=tab[:, 128:256], in_=tab[:, 0:128])
             nc.scalar.copy(out=tab[:, 256:512], in_=tab[:, 0:256])
 
-        def multiply(acc, g, codes, col0):
+        def multiply(acc, g, codes, col0, width=BLOCK):
             nc.tensor.matmul_mx(
                 out=acc[:],
                 lhsT=xc[:, g, :].bitcast(FP4X4),
                 lhsT_scale=xs[:, g, :],
                 rhs=codes.bitcast(FP4X4),
-                rhs_scale=ws[g][:, col0 : col0 + BLOCK],
+                rhs_scale=ws[g][:, col0 : col0 + width],
                 start=(g == 0),
                 stop=(g == PASSES - 1),
             )
 
-        acc = [psum.tile([P, BLOCK], F32, name="acc%d" % j) for j in range(6)]
+        acc = [psum.tile([P, BLOCK], F32, name="acc%d" % j) for j in range(5)]
+        HALF = BLOCK // 2
+        vacc = [psum.tile([P, HALF], F32, name="vacc%d" % h) for h in range(2)]
+
+        def multiply_kv(g, j):
+            if j == 4:
+                multiply(acc[4], g, wkv[(g, 4)], BLOCK * 4)
+            else:
+                for h in range(2):
+                    multiply(vacc[h], g, wkv[(g, 5)][:, 2 * HALF * h : 2 * HALF * (h + 1)], BLOCK * 5 + HALF * h, HALF)
+
         for g in range(PASSES):
             for j in range(4):
                 multiply(
@@ -150,10 +160,10 @@ def tile_rlaattention_pa_kernel(
                 )
         for g in range(KV_WHOLE):
             for j in (4, 5):
-                multiply(acc[j], g, wkv[(g, j)], BLOCK * j)
+                multiply_kv(g, j)
         for j in (4, 5):
             for g in range(KV_WHOLE, PASSES):
-                multiply(acc[j], g, wkv[(g, j)], BLOCK * j)
+                multiply_kv(g, j)
 
         res = [keep.tile([P, BLOCK], F32, name="res%d" % j, align_bytes=256) for j in range(6)]
         prods = {}
@@ -181,7 +191,9 @@ def tile_rlaattention_pa_kernel(
         combine(3)
         products(4)
         combine(4)
-        nc.scalar.copy(out=res[5][:], in_=acc[5][:])
+        nc.scalar.copy(out=res[5][:, 0:HALF], in_=vacc[0][:])
+        vres = keep.tile([P, HALF], F32, name="vres", align_bytes=256)
+        nc.vector.tensor_copy(out=vres[:], in_=vacc[1][:])
 
         def store(dst, j, queue):
             queue.dma_start(
@@ -192,4 +204,10 @@ def tile_rlaattention_pa_kernel(
         for j in range(4):
             store(out_0[0, 4 * j : 4 * j + 4], j, nc.sync)
         store(out_1[0], 4, nc.sync)
-        store(out_2[0], 5, nc.scalar)
+        nc.scalar.dma_start(
+            out=out_2[0, 0:2].rearrange("h p f -> p h f"),
+            in_=res[5][:, 0:HALF].rearrange("p (h f) -> p h f", h=2),
+        )
+        nc.sync.dma_start(
+            out=out_2[0, 2:4].rearrange("h p f -> p h f"), in_=vres[:].rearrange("p (h f) -> p h f", h=2)
+        )

@@ -70,7 +70,7 @@ def tile_rlaattention_pa_kernel(
         for t, n in enumerate(SCALE_GROUPS):
             plane = keep.tile([P, n, N_ALL], U8, name="ws%d" % t, align_bytes=256)
             nc.vector.memset(plane[:].bitcast(I32), 0)
-            for low in (0, 1, 2, 3, 32, 33, 34, 35):
+            for low in (0, 32, 1, 33, 2, 34, 3, 35):
                 for p in (low, low + 64):
                     if t == 0:
                         load_scale_row(plane, g0, n, p)

from contextlib import ExitStack

import concourse.mybir as mybir

F32 = mybir.dt.float32
BF16 = mybir.dt.bfloat16
U8 = mybir.dt.uint8
I32 = mybir.dt.int32
FP4X4 = mybir.dt.float4_e2m1fn_x4
MULT = mybir.AluOpType.mult
ADD = mybir.AluOpType.add

P = 128
PASSES = 16
N_ALL = 3072
BLOCK = 512
Q_COLS = 2048
KV_COLS = 1024

FLOPS = 2 * 128 * 8192 * 3072

SCALE_GROUPS = (8, 8)
Q_LOAD_PASSES = 1
KV_WHOLE = 10
LATE_LOADS = (3, 2, 1)


def tile_rlaattention_pa_kernel(
    tc, x_words, x_scales, freqs_cis, Wqkv_words, Wqkv_scales, out_0, out_1, out_2
):
    nc = tc.nc
    with ExitStack() as ctx:
        keep = ctx.enter_context(tc.tile_pool(name="keep", bufs=1))
        work = ctx.enter_context(tc.tile_pool(name="work", bufs=3))
        psum = ctx.enter_context(tc.psum_pool(name="psum", bufs=1))

        fr = keep.tile([P, 128], BF16, name="fr", align_bytes=256)
        nc.scalar.dma_start(out=fr[:], in_=freqs_cis)

        xc = keep.tile([P, PASSES, 256], U8, name="xc", align_bytes=256)
        nc.sync.dma_start(
            out=xc[:].bitcast(I32), in_=x_words.rearrange("g p n -> p g n").bitcast(I32)
        )

        def load_scale_rows(plane, rows, apart):
            nc.vector.memset(plane[:].bitcast(I32), 0)
            for quad in range(apart // 32):
                for r in range(4):
                    nc.sync.dma_start(
                        out=plane[32 * quad + r : P : apart, :, :].bitcast(I32),
                        in_=rows[:, 4 * quad + r : 16 : apart // 8, :]
                        .rearrange("g q n -> q g n")
                        .bitcast(I32),
                    )

        xs = keep.tile([P, PASSES, 128], U8, name="xs", align_bytes=256)
        load_scale_rows(xs, x_scales, 32)

        ws = {}
        woven = []

        def load_scale_row(plane, g0, n, p):
            q = 4 * (p // 32) + p % 32
            nc.sync.dma_start(
                out=plane[p : p + 1, :, :].bitcast(I32),
                in_=Wqkv_scales[g0 : g0 + n, q : q + 1, :].rearrange("g q n -> q g n").bitcast(I32),
            )

        g0 = 0
        for t, n in enumerate(SCALE_GROUPS):
            plane = keep.tile([P, n, N_ALL], U8, name="ws%d" % t, align_bytes=256)
            nc.vector.memset(plane[:].bitcast(I32), 0)
            for low in (0, 32, 1, 33, 2, 34, 3, 35):
                for p in (low, low + 64):
                    if t == 0:
                        load_scale_row(plane, g0, n, p)
                    else:
                        woven.append((plane, g0, n, p))
            for s in range(n):
                ws[g0 + s] = plane[:, s, :]
            g0 += n

        wq = []
        for i in range(PASSES // Q_LOAD_PASSES):
            codes = keep.tile([P, Q_LOAD_PASSES, 2 * Q_COLS], U8, name="wq%d" % i, align_bytes=256)
            nc.sync.dma_start(
                out=codes[:].bitcast(I32),
                in_=Wqkv_words[i * Q_LOAD_PASSES : (i + 1) * Q_LOAD_PASSES, :, 0 : 2 * Q_COLS]
                .rearrange("g p n -> p g n")
                .bitcast(I32),
            )
            wq.append(codes)
            for item in woven[2 * i : 2 * i + 2]:
                load_scale_row(*item)

        wkv = {}
        for g in range(KV_WHOLE):
            codes = keep.tile([P, 2 * KV_COLS], U8, name="wkv%d" % g, align_bytes=256)
            nc.sync.dma_start(
                out=codes[:].bitcast(I32), in_=Wqkv_words[g, :, 2 * Q_COLS : 2 * N_ALL].bitcast(I32)
            )
            for j in (4, 5):
                wkv[(g, j)] = codes[:, 2 * BLOCK * (j - 4) : 2 * BLOCK * (j - 3)]
        for j in (4, 5):
            g0 = KV_WHOLE
            for n in LATE_LOADS:
                codes = keep.tile([P, n, 2 * BLOCK], U8, name="late%d_%d" % (j, g0), align_bytes=256)
                nc.sync.dma_start(
                    out=codes[:].bitcast(I32),
                    in_=Wqkv_words[g0 : g0 + n, :, 2 * BLOCK * j : 2 * BLOCK * (j + 1)]
                    .rearrange("g p n -> p g n")
                    .bitcast(I32),
                )
                for s in range(n):
                    wkv[(g0 + s, j)] = codes[:, s, :]
                g0 += n

        fa = keep.tile([P, BLOCK], F32, name="fa")
        fb = keep.tile([P, BLOCK], F32, name="fb")
        fr3 = fr[:].rearrange("p (j t) -> p j t", t=2)
        fa3 = fa[:, 0:128].rearrange("p (j t) -> p j t", t=2)
        fb3 = fb[:, 0:128].rearrange("p (j t) -> p j t", t=2)
        nc.scalar.copy(out=fa3[:, :, 0], in_=fr3[:, :, 1])
        nc.scalar.copy(out=fa3[:, :, 1], in_=fr3[:, :, 1])
        nc.scalar.copy(out=fb3[:, :, 0], in_=fr3[:, :, 0])
        nc.scalar.mul(out=fb3[:, :, 1], in_=fr3[:, :, 0], mul=-1.0)
        for tab in (fa, fb):
            nc.scalar.copy(out=tab[:, 128:256], in_=tab[:, 0:128])
            nc.scalar.copy(out=tab[:, 256:512], in_=tab[:, 0:256])

        def multiply(acc, g, codes, col0, width=BLOCK):
            nc.tensor.matmul_mx(
                out=acc[:],
                lhsT=xc[:, g, :].bitcast(FP4X4),
                lhsT_scale=xs[:, g, :],
                rhs=codes.bitcast(FP4X4),
                rhs_scale=ws[g][:, col0 : col0 + width],
                start=(g == 0),
                stop=(g == PASSES - 1),
            )

        acc = [psum.tile([P, BLOCK], F32, name="acc%d" % j) for j in range(5)]
        HALF = BLOCK // 2
        vacc = [psum.tile([P, HALF], F32, name="vacc%d" % h) for h in range(2)]

        def multiply_kv(g, j):
            if j == 4:
                multiply(acc[4], g, wkv[(g, 4)], BLOCK * 4)
            else:
                for h in range(2):
                    multiply(vacc[h], g, wkv[(g, 5)][:, 2 * HALF * h : 2 * HALF * (h + 1)], BLOCK * 5 + HALF * h, HALF)

        for g in range(PASSES):
            for j in range(4):
                multiply(
                    acc[j],
                    g,
                    wq[g // Q_LOAD_PASSES][:, g % Q_LOAD_PASSES, 2 * BLOCK * j : 2 * BLOCK * (j + 1)],
                    BLOCK * j,
                )
        for g in range(KV_WHOLE):
            for j in (4, 5):
                multiply_kv(g, j)
        for j in (4, 5):
            for g in range(KV_WHOLE, PASSES):
                multiply_kv(g, j)

        res = [keep.tile([P, BLOCK], F32, name="res%d" % j, align_bytes=256) for j in range(6)]
        prods = {}

        def products(j):
            m1 = work.tile([P, BLOCK], F32, name="m1")
            m2 = work.tile([P, BLOCK], F32, name="m2")
            nc.vector.tensor_tensor(out=m1[:], in0=acc[j][:], in1=fa[:], op=MULT)
            nc.vector.tensor_tensor(out=m2[:], in0=acc[j][:], in1=fb[:], op=MULT)
            prods[j] = (m1, m2)

        def combine(j):
            m1, m2 = prods[j]
            nc.vector.tensor_tensor(
                out=res[j][:].rearrange("p (j t) -> p j t", t=2),
                in0=m1[:].rearrange("p (j t) -> p j t", t=2),
                in1=m2[:].rearrange("p (j t) -> p j t", t=2)[:, :, ::-1],
                op=ADD,
            )

        products(0)
        for j in range(1, 4):
            products(j)
            combine(j - 1)
        combine(3)
        products(4)
        combine(4)
        nc.scalar.copy(out=res[5][:, 0:HALF], in_=vacc[0][:])
        vres = keep.tile([P, HALF], F32, name="vres", align_bytes=256)
        nc.vector.tensor_copy(out=vres[:], in_=vacc[1][:])

        def store(dst, j, queue):
            queue.dma_start(
                out=dst.rearrange("h p f -> p h f"),
                in_=res[j][:].rearrange("p (h f) -> p h f", h=4),
            )

        for j in range(4):
            store(out_0[0, 4 * j : 4 * j + 4], j, nc.sync)
        store(out_1[0], 4, nc.sync)
        nc.scalar.dma_start(
            out=out_2[0, 0:2].rearrange("h p f -> p h f"),
            in_=res[5][:, 0:HALF].rearrange("p (h f) -> p h f", h=2),
        )
        nc.sync.dma_start(
            out=out_2[0, 2:4].rearrange("h p f -> p h f"), in_=vres[:].rearrange("p (h f) -> p h f", h=2)
        )
